import numpy as np
import ml_dtypes


def mxq(x, axis, fmt="e4m3"):
    dtype, down = {"e4m3": (ml_dtypes.float8_e4m3fn, 7), "e5m2": (ml_dtypes.float8_e5m2, 14)}[fmt]
    v = np.moveaxis(np.asarray(x, np.float32).astype(ml_dtypes.bfloat16).astype(np.float64), axis, -1)
    blocks = v.reshape(v.shape[:-1] + (-1, 32))
    amax = np.abs(blocks).max(-1, keepdims=True)
    byte = np.maximum(np.where(amax > 0, np.frexp(amax)[1] - 1 + 127, 0) - down, 1)
    scale = np.exp2(byte - 127.0)
    codes = (blocks / scale).astype(np.float32).astype(dtype).astype(np.float64)
    return np.moveaxis((codes * scale).reshape(v.shape), -1, axis)


WIDE = False


def mx_kscale(k):
    if not WIDE:
        return np.ones(k)
    levels = np.array([10, -10, 5, -5, 0])
    a = np.random.permutation(np.resize(levels, k // 512 * 4)).reshape(k // 512, 4)
    idx = np.arange(k)
    return np.exp2(a[idx // 512, idx % 128 // 32])


BF16 = ml_dtypes.bfloat16


def bf(x):
    return np.asarray(x, np.float32).astype(BF16)


def f64(x):
    return np.asarray(x).astype(np.float64)


E2M1 = np.array([0.0, 0.5, 1.0, 1.5, 2.0, 3.0, 4.0, 6.0, -0.0, -0.5, -1.0, -1.5, -2.0, -3.0, -4.0, -6.0])


def pack_weight(w, fmt):
    k, n = w.shape
    w = f64(bf(w)).reshape(k // 32, 32, n)
    amax = np.abs(w).max(1)
    if fmt == "e4m3":
        byte = np.frexp(amax)[1] - 1 + 127 - 7
    else:
        mant, ex = np.frexp(amax / 6.0)
        byte = np.where(mant > 0.5, ex, ex - 1) + 127
    byte = np.clip(np.where(amax > 0, byte, 1), 1, 254)
    scaled = (w * np.exp2(127.0 - byte)[:, None, :]).reshape(k, n).astype(np.float32)
    by_word = np.ascontiguousarray(scaled.reshape(k // 512, 128, 4, n).transpose(0, 1, 3, 2))
    if fmt == "e4m3":
        words = by_word.astype(ml_dtypes.float8_e4m3fn).view(np.uint8)
    else:
        c = by_word.astype(ml_dtypes.float4_e2m1fn).view(np.uint8) & 0xF
        words = c[..., 0::2] | (c[..., 1::2] << 4)
    return np.ascontiguousarray(words), np.ascontiguousarray(byte.astype(np.uint8).reshape(k // 512, 16, n))


def unpack_weight(words, scales, fmt):
    g, p, n, _ = words.shape
    if fmt == "e4m3":
        vals = np.ascontiguousarray(words).view(ml_dtypes.float8_e4m3fn).astype(np.float64)
    else:
        nib = np.empty((g, p, n, 4), np.uint8)
        nib[..., 0::2] = words & 0xF
        nib[..., 1::2] = words >> 4
        vals = E2M1[nib]
    vals = vals * np.repeat(np.exp2(scales.astype(np.float64) - 127.0), 8, axis=1)[..., None]
    return vals.transpose(0, 1, 3, 2).reshape(g * 512, n)


B, N, P, D, H = 8, 512, 4, 128, 2
E = P * D
DH = E // H
FMT = "e4m3"


def sincos_table(n, e):
    pe = np.zeros((n, e))
    position = np.arange(n, dtype=np.float64)[:, None]
    div_term = np.exp(np.arange(0, e, 2, dtype=np.float64) * -(np.log(10000.0) / e))
    pe[:, 0::2] = np.sin(position * div_term)
    pe[:, 1::2] = np.cos(position * div_term)
    pe = pe - pe.mean()
    return pe / (pe.std() * 10)


def setup_inputs():
    s, t = mx_kscale(E), mx_kscale(E)
    c = 1.0 / np.sqrt(E)
    x = bf(np.random.standard_normal((B, N, P, D)) * s.reshape(P, D))
    pos_embed = bf(sincos_table(N, E) * t)
    W_embed_words, W_embed_scales = pack_weight((np.random.standard_normal((E, E)) * c * t[:, None] / s).T, FMT)
    b_embed = bf(np.random.standard_normal(E) * 0.1 * t)
    Wq_words, Wq_scales = pack_weight((np.random.standard_normal((E, E)) * c / t).T, FMT)
    bq = bf(np.random.standard_normal(E) * 0.1)
    Wk_words, Wk_scales = pack_weight((np.random.standard_normal((E, E)) * c / t).T, FMT)
    bk = bf(np.random.standard_normal(E) * 0.1)
    Wv_words, Wv_scales = pack_weight((np.random.standard_normal((E, E)) * c / t).T, FMT)
    bv = bf(np.random.standard_normal(E) * 0.1)
    return {"x": x,
            "pos_embed": pos_embed,
            "W_embed_words": W_embed_words,
            "W_embed_scales": W_embed_scales,
            "b_embed": b_embed,
            "Wq_words": Wq_words,
            "Wq_scales": Wq_scales,
            "bq": bq,
            "Wk_words": Wk_words,
            "Wk_scales": Wk_scales,
            "bk": bk,
            "Wv_words": Wv_words,
            "Wv_scales": Wv_scales,
            "bv": bv}


def reference(x, pos_embed, W_embed_words, W_embed_scales, b_embed, Wq_words, Wq_scales, bq, Wk_words, Wk_scales, bk, Wv_words, Wv_scales, bv):
    xf = f64(x).reshape(B, N, E)
    xe = (mxq(xf, 2, "e4m3") @ unpack_weight(W_embed_words, W_embed_scales, FMT)) + f64(b_embed)
    xe = xe + f64(pos_embed)
    xq = mxq(xe, 2, "e4m3")
    q = ((xq @ unpack_weight(Wq_words, Wq_scales, FMT)) + f64(bq)).reshape(B, N, H, DH)
    k = ((xq @ unpack_weight(Wk_words, Wk_scales, FMT)) + f64(bk)).reshape(B, N, H, DH)
    v = ((xq @ unpack_weight(Wv_words, Wv_scales, FMT)) + f64(bv)).reshape(B, N, H, DH)
    return q, k, v

@@ -1,0 +1,208 @@
+from contextlib import ExitStack
+
+import concourse.mybir as mybir
+from concourse.masks import make_identity
+
+F32 = mybir.dt.float32
+BF16 = mybir.dt.bfloat16
+I32 = mybir.dt.int32
+U32 = mybir.dt.uint32
+U8 = mybir.dt.uint8
+FP8X4 = mybir.dt.float8_e4m3fn_x4
+ADD = mybir.AluOpType.add
+
+P = 128
+BATCHES = 8
+POSITIONS = 512
+WIDTH = 512
+TILES = POSITIONS // P
+PAIR = 2
+UNITS = BATCHES * TILES // PAIR
+HALVES = 2
+WEIGHTS = 4
+
+FLOPS = WEIGHTS * 2 * BATCHES * POSITIONS * WIDTH * WIDTH
+
+
+def tile_attention_pa_t_kernel(
+    tc,
+    x,
+    pos_embed,
+    W_embed_words,
+    W_embed_scales,
+    b_embed,
+    Wq_words,
+    Wq_scales,
+    bq,
+    Wk_words,
+    Wk_scales,
+    bk,
+    Wv_words,
+    Wv_scales,
+    bv,
+    out_0,
+    out_1,
+    out_2,
+):
+    nc = tc.nc
+    words_in = [W_embed_words, Wq_words, Wk_words, Wv_words]
+    scales_in = [W_embed_scales, Wq_scales, Wk_scales, Wv_scales]
+    biases_in = [b_embed, bq, bk, bv]
+    x_rows = x.rearrange("b (p i) c d -> b p i (c d)", i=TILES)
+    pos_rows = pos_embed.rearrange("(p i) e -> p i e", i=TILES)
+    out_rows = [o.rearrange("b (p i) h d -> b p i (h d)", i=TILES) for o in (out_0, out_1, out_2)]
+
+    with ExitStack() as stack:
+        stack.enter_context(tc.manual_schedule())
+        keep = stack.enter_context(tc.tile_pool(name="keep", bufs=1))
+        work = stack.enter_context(tc.tile_pool(name="work", bufs=2))
+        results = stack.enter_context(tc.tile_pool(name="results", bufs=3))
+        psum_t = stack.enter_context(tc.psum_pool(name="psum_t", bufs=2))
+        psum_xe = stack.enter_context(tc.psum_pool(name="psum_xe", bufs=2))
+        psum_qkv = stack.enter_context(tc.psum_pool(name="psum_qkv", bufs=4))
+
+        w_words = keep.tile([P, WEIGHTS, WIDTH], U32, align_bytes=64)
+        w_scales = keep.tile([P, WEIGHTS, WIDTH], U8, align_bytes=64)
+        bias_rows = keep.tile([P, WEIGHTS, WIDTH], BF16)
+        ones = keep.tile([P, P], BF16)
+        ident = keep.tile([P, P], F32)
+        pos_sb = keep.tile([P, TILES, WIDTH], BF16)
+        nc.vector.memset(w_scales[:].bitcast(I32), 0)
+        nc.vector.memset(bias_rows[:], 0.0)
+        nc.vector.memset(ones[:], 1.0)
+        make_identity(nc, ident[:])
+
+        def load_scales(w):
+            for quadrant in range(4):
+                nc.sync.dma_start(
+                    out=w_scales[32 * quadrant : 32 * quadrant + 4, w, :].bitcast(I32),
+                    in_=scales_in[w][0, 4 * quadrant : 4 * quadrant + 4, :].bitcast(I32),
+                )
+
+        def load_words(w):
+            nc.sync.dma_start(
+                out=w_words[:, w, :].bitcast(I32),
+                in_=words_in[w][0].rearrange("p n t -> p (n t)").bitcast(I32),
+            )
+
+        x_sb = []
+        for b in range(BATCHES):
+            x_batch = keep.tile([P, TILES, WIDTH], BF16, name="x_batch%d" % b)
+            x_sb.append(x_batch)
+
+        nc.sync.dma_start(out=x_sb[0][:], in_=x_rows[0])
+        load_scales(0)
+        load_words(0)
+        for w in range(WEIGHTS):
+            nc.sync.dma_start(out=bias_rows[0:1, w, :], in_=biases_in[w].unsqueeze(0))
+        nc.sync.dma_start(out=pos_sb[:], in_=pos_rows)
+        for w in range(1, WEIGHTS):
+            load_scales(w)
+        for w in range(1, WEIGHTS):
+            load_words(w)
+        for b in range(1, BATCHES):
+            nc.sync.dma_start(out=x_sb[b][:], in_=x_rows[b])
+
+        def words_to_codes(token_words, kind):
+            flipped = psum_t.tile([P, PAIR, HALVES, P], F32, tag="flipped")
+            for j in range(PAIR):
+                for u in range(HALVES):
+                    nc.tensor.transpose(flipped[:, j, u, :], token_words(j, u), ident[:])
+            grouped = work.tile([P, PAIR, P, 2 * HALVES], BF16, tag=kind + "_grouped", align_bytes=64)
+            nc.scalar.copy(out=grouped[:].bitcast(F32), in_=flipped[:].rearrange("q j u m -> q j m u"))
+            codes = work.tile([P, PAIR * P], U32, tag=kind + "_codes", align_bytes=64)
+            scales = work.tile([P, PAIR * P], U8, tag=kind + "_scales", align_bytes=64)
+            nc.vector.quantize_mx(
+                out=codes[:].bitcast(FP8X4),
+                scales=scales[:],
+                in_=grouped[:].rearrange("q j m t -> q (j m t)"),
+            )
+            return codes, scales
+
+        def mx_pass(acc, codes, scales, j, w):
+            tokens = slice(j * P, (j + 1) * P)
+            nc.tensor.matmul_mx(
+                out=acc[:],
+                lhsT=codes[:, tokens].bitcast(FP8X4),
+                lhsT_scale=scales[:, tokens],
+                rhs=w_words[:, w, :].bitcast(FP8X4),
+                rhs_scale=w_scales[:, w, :],
+                start=True,
+                stop=True,
+            )
+
+        x_mx = {}
+        xe_mx = {}
+        xe_sb = {}
+
+        def quantise_x(unit):
+            x_words = x_sb[unit // 2][:].bitcast(F32)
+            first = PAIR * (unit % 2)
+            x_mx[unit] = words_to_codes(lambda j, u: x_words[:, first + j, u : WIDTH // 2 : HALVES], "x")
+
+        def embed(unit):
+            codes, scales = x_mx[unit]
+            first = PAIR * (unit % 2)
+            xe_pair = work.tile([P, PAIR, WIDTH], BF16, tag="xe_pair")
+            for j in range(PAIR):
+                xe_acc = psum_xe.tile([P, WIDTH], F32, tag="xe_acc")
+                mx_pass(xe_acc, codes, scales, j, 0)
+                nc.vector.tensor_tensor(
+                    out=xe_pair[:, j, :].rearrange("m (u q e) -> m u q e", u=HALVES, e=2),
+                    in0=xe_acc[:].rearrange("m (q u e) -> m u q e", u=HALVES, e=2),
+                    in1=pos_bias[:, first + j, :].rearrange("m (u q e) -> m u q e", u=HALVES, e=2),
+                    op=ADD,
+                )
+            xe_sb[unit] = xe_pair
+
+        def quantise_xe(unit):
+            xe_words = xe_sb[unit][:].bitcast(F32)
+            xe_mx[unit] = words_to_codes(lambda j, u: xe_words[:, j, u * P : (u + 1) * P], "xe")
+
+        def project(unit):
+            codes, scales = xe_mx[unit]
+            first = PAIR * (unit % 2)
+            q_sb = results.tile([P, PAIR, WIDTH], F32, tag="q_sb")
+            k_sb = results.tile([P, PAIR, WIDTH], F32, tag="k_sb")
+            v_sb = results.tile([P, PAIR, WIDTH], F32, tag="v_sb")
+            for j in range(PAIR):
+                for w, dest in ((1, q_sb), (2, k_sb)):
+                    acc = psum_qkv.tile([P, WIDTH], F32, tag="acc")
+                    mx_pass(acc, codes, scales, j, w)
+                    nc.vector.tensor_tensor(out=dest[:, j, :], in0=acc[:], in1=bias_sb[:, w, :], op=ADD)
+                acc = psum_qkv.tile([P, WIDTH], F32, tag="acc")
+                mx_pass(acc, codes, scales, j, 3)
+                nc.scalar.copy(out=v_sb[:, j, :], in_=acc[:])
+            nc.gpsimd.tensor_tensor(
+                out=v_sb[:],
+                in0=v_sb[:],
+                in1=bias_sb[:, 3, :].unsqueeze(1).to_broadcast([P, PAIR, WIDTH]),
+                op=ADD,
+            )
+            for rows, dest in zip(out_rows, (q_sb, k_sb, v_sb)):
+                nc.sync.dma_start(out=rows[unit // 2][:, first : first + PAIR, :], in_=dest[:])
+
+        quantise_x(0)
+        bias_sb = keep.tile([P, WEIGHTS, WIDTH], F32)
+        for w in range(WEIGHTS):
+            spread = psum_qkv.tile([P, WIDTH], F32, tag="acc")
+            nc.tensor.matmul(out=spread[:], lhsT=ones[:], rhs=bias_rows[:, w, :], start=True, stop=True)
+            nc.scalar.copy(out=bias_sb[:, w, :], in_=spread[:])
+        pos_bias = keep.tile([P, TILES, WIDTH], F32)
+        for i in range(TILES):
+            nc.vector.tensor_tensor(
+                out=pos_bias[:, i, :].rearrange("m (u q e) -> m u q e", u=HALVES, e=2),
+                in0=pos_sb[:, i, :].rearrange("m (q u e) -> m u q e", u=HALVES, e=2),
+                in1=bias_sb[:, 0, :].rearrange("m (q u e) -> m u q e", u=HALVES, e=2),
+                op=ADD,
+            )
+
+        for step in range(-2, UNITS):
+            if 0 < step + 3 < UNITS:
+                quantise_x(step + 3)
+            if 0 <= step + 1 < UNITS:
+                quantise_xe(step + 1)
+            if 0 <= step + 2 < UNITS:
+                embed(step + 2)
+            if 0 <= step:
+                project(step)

@@ -56,7 +56,7 @@ def tile_attention_pa_t_kernel(
         stack.enter_context(tc.manual_schedule())
         keep = stack.enter_context(tc.tile_pool(name="keep", bufs=1))
         work = stack.enter_context(tc.tile_pool(name="work", bufs=2))
-        results = stack.enter_context(tc.tile_pool(name="results", bufs=3))
+        results = stack.enter_context(tc.tile_pool(name="results", bufs=4))
         psum_t = stack.enter_context(tc.psum_pool(name="psum_t", bufs=2))
         psum_xe = stack.enter_context(tc.psum_pool(name="psum_xe", bufs=2))
         psum_qkv = stack.enter_context(tc.psum_pool(name="psum_qkv", bufs=4))
@@ -103,13 +103,16 @@ def tile_attention_pa_t_kernel(
         for b in range(1, BATCHES):
             nc.sync.dma_start(out=x_sb[b][:], in_=x_rows[b])
 
-        def words_to_codes(token_words, kind):
+        def flip(token_words, kind):
             flipped = psum_t.tile([P, PAIR, HALVES, P], F32, tag="flipped")
             for j in range(PAIR):
                 for u in range(HALVES):
                     nc.tensor.transpose(flipped[:, j, u, :], token_words(j, u), ident[:])
             grouped = work.tile([P, PAIR, P, 2 * HALVES], BF16, tag=kind + "_grouped", align_bytes=64)
             nc.scalar.copy(out=grouped[:].bitcast(F32), in_=flipped[:].rearrange("q j u m -> q j m u"))
+            return grouped
+
+        def quantise(grouped, kind):
             codes = work.tile([P, PAIR * P], U32, tag=kind + "_codes", align_bytes=64)
             scales = work.tile([P, PAIR * P], U8, tag=kind + "_scales", align_bytes=64)
             nc.vector.quantize_mx(
@@ -119,7 +122,8 @@ def tile_attention_pa_t_kernel(
             )
             return codes, scales
 
-        def mx_pass(acc, codes, scales, j, w):
+        def mx_pass(acc, operand, j, w):
+            codes, scales = operand
             tokens = slice(j * P, (j + 1) * P)
             nc.tensor.matmul_mx(
                 out=acc[:],
@@ -131,22 +135,24 @@ def tile_attention_pa_t_kernel(
                 stop=True,
             )
 
+        x_grouped = {}
         x_mx = {}
-        xe_mx = {}
         xe_sb = {}
+        xe_grouped = {}
+        xe_mx = {}
+        qkv_sb = {}
 
-        def quantise_x(unit):
+        def flip_x(unit):
             x_words = x_sb[unit // 2][:].bitcast(F32)
             first = PAIR * (unit % 2)
-            x_mx[unit] = words_to_codes(lambda j, u: x_words[:, first + j, u : WIDTH // 2 : HALVES], "x")
+            x_grouped[unit] = flip(lambda j, u: x_words[:, first + j, u : WIDTH // 2 : HALVES], "x")
 
         def embed(unit):
-            codes, scales = x_mx[unit]
             first = PAIR * (unit % 2)
             xe_pair = work.tile([P, PAIR, WIDTH], BF16, tag="xe_pair")
             for j in range(PAIR):
                 xe_acc = psum_xe.tile([P, WIDTH], F32, tag="xe_acc")
-                mx_pass(xe_acc, codes, scales, j, 0)
+                mx_pass(xe_acc, x_mx[unit], j, 0)
                 nc.vector.tensor_tensor(
                     out=xe_pair[:, j, :].rearrange("m (u q e) -> m u q e", u=HALVES, e=2),
                     in0=xe_acc[:].rearrange("m (q u e) -> m u q e", u=HALVES, e=2),
@@ -155,34 +161,39 @@ def tile_attention_pa_t_kernel(
                 )
             xe_sb[unit] = xe_pair
 
-        def quantise_xe(unit):
+        def flip_xe(unit):
             xe_words = xe_sb[unit][:].bitcast(F32)
-            xe_mx[unit] = words_to_codes(lambda j, u: xe_words[:, j, u * P : (u + 1) * P], "xe")
+            xe_grouped[unit] = flip(lambda j, u: xe_words[:, j, u * P : (u + 1) * P], "xe")
 
-        def project(unit):
-            codes, scales = xe_mx[unit]
-            first = PAIR * (unit % 2)
-            q_sb = results.tile([P, PAIR, WIDTH], F32, tag="q_sb")
-            k_sb = results.tile([P, PAIR, WIDTH], F32, tag="k_sb")
-            v_sb = results.tile([P, PAIR, WIDTH], F32, tag="v_sb")
-            for j in range(PAIR):
-                for w, dest in ((1, q_sb), (2, k_sb)):
-                    acc = psum_qkv.tile([P, WIDTH], F32, tag="acc")
-                    mx_pass(acc, codes, scales, j, w)
-                    nc.vector.tensor_tensor(out=dest[:, j, :], in0=acc[:], in1=bias_sb[:, w, :], op=ADD)
+        def project(unit, j):
+            if j == 0:
+                q_sb = results.tile([P, PAIR, WIDTH], F32, tag="q_sb")
+                k_sb = results.tile([P, PAIR, WIDTH], F32, tag="k_sb")
+                v_sb = results.tile([P, PAIR, WIDTH], F32, tag="v_sb")
+                qkv_sb[unit] = (q_sb, k_sb, v_sb)
+            q_sb, k_sb, v_sb = qkv_sb[unit]
+            for w, dest in ((1, q_sb), (2, k_sb)):
                 acc = psum_qkv.tile([P, WIDTH], F32, tag="acc")
-                mx_pass(acc, codes, scales, j, 3)
-                nc.scalar.copy(out=v_sb[:, j, :], in_=acc[:])
+                mx_pass(acc, xe_mx[unit], j, w)
+                nc.vector.tensor_tensor(out=dest[:, j, :], in0=acc[:], in1=bias_sb[:, w, :], op=ADD)
+            acc = psum_qkv.tile([P, WIDTH], F32, tag="acc")
+            mx_pass(acc, xe_mx[unit], j, 3)
+            nc.scalar.copy(out=v_sb[:, j, :], in_=acc[:])
+
+        def store(unit):
+            first = PAIR * (unit % 2)
+            v_sb = qkv_sb[unit][2]
             nc.gpsimd.tensor_tensor(
                 out=v_sb[:],
                 in0=v_sb[:],
                 in1=bias_sb[:, 3, :].unsqueeze(1).to_broadcast([P, PAIR, WIDTH]),
                 op=ADD,
             )
-            for rows, dest in zip(out_rows, (q_sb, k_sb, v_sb)):
+            for rows, dest in zip(out_rows, qkv_sb[unit]):
                 nc.sync.dma_start(out=rows[unit // 2][:, first : first + PAIR, :], in_=dest[:])
 
-        quantise_x(0)
+        flip_x(0)
+        x_mx[0] = quantise(x_grouped[0], "x")
         bias_sb = keep.tile([P, WEIGHTS, WIDTH], F32)
         for w in range(WEIGHTS):
             spread = psum_qkv.tile([P, WIDTH], F32, tag="acc")
@@ -198,11 +209,19 @@ def tile_attention_pa_t_kernel(
             )
 
         for step in range(-2, UNITS):
-            if 0 < step + 3 < UNITS:
-                quantise_x(step + 3)
-            if 0 <= step + 1 < UNITS:
-                quantise_xe(step + 1)
-            if 0 <= step + 2 < UNITS:
-                embed(step + 2)
+            ahead_x, ahead_embed, ahead_xe = step + 3, step + 2, step + 1
+            if ahead_x < UNITS:
+                flip_x(ahead_x)
+            if 0 <= ahead_xe < UNITS:
+                flip_xe(ahead_xe)
             if 0 <= step:
-                project(step)
+                project(step, 0)
+            if ahead_x < UNITS:
+                x_mx[ahead_x] = quantise(x_grouped[ahead_x], "x")
+            if 0 <= ahead_xe < UNITS:
+                xe_mx[ahead_xe] = quantise(xe_grouped[ahead_xe], "xe")
+            if 0 <= ahead_embed < UNITS:
+                embed(ahead_embed)
+            if 0 <= step:
+                project(step, 1)
+                store(step)

@@ -20,6 +20,8 @@ PAIR = 2
 UNITS = BATCHES * TILES // PAIR
 HALVES = 2
 WEIGHTS = 4
+OUTPUTS = 3
+V_OUT = 2
 
 FLOPS = WEIGHTS * 2 * BATCHES * POSITIONS * WIDTH * WIDTH
 
@@ -90,12 +92,16 @@ def tile_attention_pa_t_kernel(
             x_batch = keep.tile([P, TILES, WIDTH], BF16, name="x_batch%d" % b)
             x_sb.append(x_batch)
 
-        nc.sync.dma_start(out=x_sb[0][:], in_=x_rows[0])
+        first_pair = slice(0, PAIR)
+        second_pair = slice(PAIR, TILES)
+        nc.sync.dma_start(out=x_sb[0][:, first_pair, :], in_=x_rows[0][:, first_pair, :])
         load_scales(0)
         load_words(0)
         for w in range(WEIGHTS):
             nc.sync.dma_start(out=bias_rows[0:1, w, :], in_=biases_in[w].unsqueeze(0))
-        nc.sync.dma_start(out=pos_sb[:], in_=pos_rows)
+        nc.sync.dma_start(out=pos_sb[:, first_pair, :], in_=pos_rows[:, first_pair, :])
+        nc.sync.dma_start(out=x_sb[0][:, second_pair, :], in_=x_rows[0][:, second_pair, :])
+        nc.sync.dma_start(out=pos_sb[:, second_pair, :], in_=pos_rows[:, second_pair, :])
         for w in range(1, WEIGHTS):
             load_scales(w)
         for w in range(1, WEIGHTS):
@@ -165,48 +171,53 @@ def tile_attention_pa_t_kernel(
             xe_words = xe_sb[unit][:].bitcast(F32)
             xe_grouped[unit] = flip(lambda j, u: xe_words[:, j, u * P : (u + 1) * P], "xe")
 
-        def project(unit, j):
-            if j == 0:
+        def project(unit, j, o):
+            if unit not in qkv_sb:
                 q_sb = results.tile([P, PAIR, WIDTH], F32, tag="q_sb")
                 k_sb = results.tile([P, PAIR, WIDTH], F32, tag="k_sb")
                 v_sb = results.tile([P, PAIR, WIDTH], F32, tag="v_sb")
                 qkv_sb[unit] = (q_sb, k_sb, v_sb)
-            q_sb, k_sb, v_sb = qkv_sb[unit]
-            for w, dest in ((1, q_sb), (2, k_sb)):
-                acc = psum_qkv.tile([P, WIDTH], F32, tag="acc")
-                mx_pass(acc, xe_mx[unit], j, w)
-                nc.vector.tensor_tensor(out=dest[:, j, :], in0=acc[:], in1=bias_sb[:, w, :], op=ADD)
+            dest = qkv_sb[unit][o]
             acc = psum_qkv.tile([P, WIDTH], F32, tag="acc")
-            mx_pass(acc, xe_mx[unit], j, 3)
-            nc.scalar.copy(out=v_sb[:, j, :], in_=acc[:])
+            mx_pass(acc, xe_mx[unit], j, 1 + o)
+            if o == V_OUT:
+                nc.scalar.copy(out=dest[:, j, :], in_=acc[:])
+            else:
+                nc.vector.tensor_tensor(out=dest[:, j, :], in0=acc[:], in1=bias_sb[:, o, :], op=ADD)
 
         def store(unit):
             first = PAIR * (unit % 2)
-            v_sb = qkv_sb[unit][2]
+            v_sb = qkv_sb[unit][V_OUT]
             nc.gpsimd.tensor_tensor(
                 out=v_sb[:],
                 in0=v_sb[:],
-                in1=bias_sb[:, 3, :].unsqueeze(1).to_broadcast([P, PAIR, WIDTH]),
+                in1=bias_sb[:, V_OUT, :].unsqueeze(1).to_broadcast([P, PAIR, WIDTH]),
                 op=ADD,
             )
             for rows, dest in zip(out_rows, qkv_sb[unit]):
                 nc.sync.dma_start(out=rows[unit // 2][:, first : first + PAIR, :], in_=dest[:])
 
-        flip_x(0)
-        x_mx[0] = quantise(x_grouped[0], "x")
-        bias_sb = keep.tile([P, WEIGHTS, WIDTH], F32)
-        for w in range(WEIGHTS):
-            spread = psum_qkv.tile([P, WIDTH], F32, tag="acc")
-            nc.tensor.matmul(out=spread[:], lhsT=ones[:], rhs=bias_rows[:, w, :], start=True, stop=True)
-            nc.scalar.copy(out=bias_sb[:, w, :], in_=spread[:])
+        def spread(w):
+            everywhere = psum_qkv.tile([P, WIDTH], F32, tag="acc")
+            nc.tensor.matmul(out=everywhere[:], lhsT=ones[:], rhs=bias_rows[:, w, :], start=True, stop=True)
+            return everywhere
+
         pos_bias = keep.tile([P, TILES, WIDTH], F32)
-        for i in range(TILES):
+        bias_sb = keep.tile([P, OUTPUTS, WIDTH], F32)
+
+        def add_b_embed(i):
             nc.vector.tensor_tensor(
                 out=pos_bias[:, i, :].rearrange("m (u q e) -> m u q e", u=HALVES, e=2),
-                in0=pos_sb[:, i, :].rearrange("m (q u e) -> m u q e", u=HALVES, e=2),
-                in1=bias_sb[:, 0, :].rearrange("m (q u e) -> m u q e", u=HALVES, e=2),
+                in0=b_embed_everywhere[:].rearrange("m (q u e) -> m u q e", u=HALVES, e=2),
+                in1=pos_sb[:, i, :].rearrange("m (q u e) -> m u q e", u=HALVES, e=2),
                 op=ADD,
             )
+
+        flip_x(0)
+        x_mx[0] = quantise(x_grouped[0], "x")
+        b_embed_everywhere = spread(0)
+        for i in range(PAIR):
+            add_b_embed(i)
 
         for step in range(-2, UNITS):
             ahead_x, ahead_embed, ahead_xe = step + 3, step + 2, step + 1
@@ -215,13 +226,20 @@ def tile_attention_pa_t_kernel(
             if 0 <= ahead_xe < UNITS:
                 flip_xe(ahead_xe)
             if 0 <= step:
-                project(step, 0)
+                for o in (0, 1, V_OUT):
+                    project(step, 0, o)
             if ahead_x < UNITS:
                 x_mx[ahead_x] = quantise(x_grouped[ahead_x], "x")
             if 0 <= ahead_xe < UNITS:
                 xe_mx[ahead_xe] = quantise(xe_grouped[ahead_xe], "xe")
             if 0 <= ahead_embed < UNITS:
                 embed(ahead_embed)
+            if ahead_embed == 0:
+                for i in range(PAIR, TILES):
+                    add_b_embed(i)
+                for o in range(OUTPUTS):
+                    nc.scalar.copy(out=bias_sb[:, o, :], in_=spread(1 + o)[:])
             if 0 <= step:
-                project(step, 1)
+                for o in (V_OUT, 0, 1):
+                    project(step, 1, o)
                 store(step)

@@ -57,7 +57,7 @@ def tile_attention_pa_t_kernel(
     with ExitStack() as stack:
         stack.enter_context(tc.manual_schedule())
         keep = stack.enter_context(tc.tile_pool(name="keep", bufs=1))
-        work = stack.enter_context(tc.tile_pool(name="work", bufs=2))
+        work = stack.enter_context(tc.tile_pool(name="work", bufs=3))
         results = stack.enter_context(tc.tile_pool(name="results", bufs=4))
         psum_t = stack.enter_context(tc.psum_pool(name="psum_t", bufs=2))
         psum_xe = stack.enter_context(tc.psum_pool(name="psum_xe", bufs=2))
@@ -185,17 +185,18 @@ def tile_attention_pa_t_kernel(
             else:
                 nc.vector.tensor_tensor(out=dest[:, j, :], in0=acc[:], in1=bias_sb[:, o, :], op=ADD)
 
-        def store(unit):
+        def finish(unit, lo, hi):
+            tiles = slice(lo, hi)
             first = PAIR * (unit % 2)
             v_sb = qkv_sb[unit][V_OUT]
             nc.gpsimd.tensor_tensor(
-                out=v_sb[:],
-                in0=v_sb[:],
-                in1=bias_sb[:, V_OUT, :].unsqueeze(1).to_broadcast([P, PAIR, WIDTH]),
+                out=v_sb[:, tiles, :],
+                in0=v_sb[:, tiles, :],
+                in1=bias_sb[:, V_OUT, :].unsqueeze(1).to_broadcast([P, hi - lo, WIDTH]),
                 op=ADD,
             )
             for rows, dest in zip(out_rows, qkv_sb[unit]):
-                nc.sync.dma_start(out=rows[unit // 2][:, first : first + PAIR, :], in_=dest[:])
+                nc.sync.dma_start(out=rows[unit // 2][:, first + lo : first + hi, :], in_=dest[:, tiles, :])
 
         def spread(w):
             everywhere = psum_qkv.tile([P, WIDTH], F32, tag="acc")
@@ -219,8 +220,9 @@ def tile_attention_pa_t_kernel(
         for i in range(PAIR):
             add_b_embed(i)
 
-        for step in range(-2, UNITS):
-            ahead_x, ahead_embed, ahead_xe = step + 3, step + 2, step + 1
+        for step in range(-3, UNITS):
+            ahead_x, ahead_embed, ahead_xe = step + 4, step + 3, step + 1
+            last = step == UNITS - 1
             if ahead_x < UNITS:
                 flip_x(ahead_x)
             if 0 <= ahead_xe < UNITS:
@@ -228,11 +230,13 @@ def tile_attention_pa_t_kernel(
             if 0 <= step:
                 for o in (0, 1, V_OUT):
                     project(step, 0, o)
+            if last:
+                finish(step, 0, 1)
             if ahead_x < UNITS:
                 x_mx[ahead_x] = quantise(x_grouped[ahead_x], "x")
             if 0 <= ahead_xe < UNITS:
                 xe_mx[ahead_xe] = quantise(xe_grouped[ahead_xe], "xe")
-            if 0 <= ahead_embed < UNITS:
+            if ahead_embed < UNITS:
                 embed(ahead_embed)
             if ahead_embed == 0:
                 for i in range(PAIR, TILES):
@@ -242,4 +246,4 @@ def tile_attention_pa_t_kernel(
             if 0 <= step:
                 for o in (V_OUT, 0, 1):
                     project(step, 1, o)
-                store(step)
+                finish(step, 1 if last else 0, PAIR)

@@ -92,22 +92,20 @@ def tile_attention_pa_t_kernel(
             x_batch = keep.tile([P, TILES, WIDTH], BF16, name="x_batch%d" % b)
             x_sb.append(x_batch)
 
-        first_pair = slice(0, PAIR)
-        second_pair = slice(PAIR, TILES)
-        nc.sync.dma_start(out=x_sb[0][:, first_pair, :], in_=x_rows[0][:, first_pair, :])
+        nc.sync.dma_start(out=x_sb[0][:], in_=x_rows[0])
         load_scales(0)
         load_words(0)
-        for w in range(WEIGHTS):
-            nc.sync.dma_start(out=bias_rows[0:1, w, :], in_=biases_in[w].unsqueeze(0))
-        nc.sync.dma_start(out=pos_sb[:, first_pair, :], in_=pos_rows[:, first_pair, :])
-        nc.sync.dma_start(out=x_sb[0][:, second_pair, :], in_=x_rows[0][:, second_pair, :])
-        nc.sync.dma_start(out=pos_sb[:, second_pair, :], in_=pos_rows[:, second_pair, :])
+        nc.sync.dma_start(out=bias_rows[0:1, 0, :], in_=biases_in[0].unsqueeze(0))
+        nc.sync.dma_start(out=pos_sb[:], in_=pos_rows)
+        for b in (1, 2):
+            nc.sync.dma_start(out=x_sb[b][:], in_=x_rows[b])
         for w in range(1, WEIGHTS):
             load_scales(w)
-        for w in range(1, WEIGHTS):
             load_words(w)
-        for b in range(1, BATCHES):
+        for b in range(3, BATCHES):
             nc.sync.dma_start(out=x_sb[b][:], in_=x_rows[b])
+        for w in range(1, WEIGHTS):
+            nc.gpsimd.dma_start(out=bias_rows[0:1, w, :], in_=biases_in[w].unsqueeze(0))
 
         def flip(token_words, kind):
             flipped = psum_t.tile([P, PAIR, HALVES, P], F32, tag="flipped")

@@ -18,10 +18,12 @@ WIDTH = 512
 TILES = POSITIONS // P
 PAIR = 2
 UNITS = BATCHES * TILES // PAIR
+PACK = 4
 HALVES = 2
 WEIGHTS = 4
 OUTPUTS = 3
 V_OUT = 2
+K_OUT = 1
 
 FLOPS = WEIGHTS * 2 * BATCHES * POSITIONS * WIDTH * WIDTH
 
@@ -69,6 +71,9 @@ def tile_attention_pa_t_kernel(
         ones = keep.tile([P, P], BF16)
         ident = keep.tile([P, P], F32)
         pos_sb = keep.tile([P, TILES, WIDTH], BF16)
+        b_embed_sb = keep.tile([P, PACK], BF16)
+        we_words = keep.tile([P, PACK, P], U32, align_bytes=64)
+        we_scales = keep.tile([P, PACK, P], U8, align_bytes=64)
         nc.vector.memset(w_scales[:].bitcast(I32), 0)
         nc.vector.memset(bias_rows[:], 0.0)
         nc.vector.memset(ones[:], 1.0)
@@ -95,7 +100,7 @@ def tile_attention_pa_t_kernel(
         nc.sync.dma_start(out=x_sb[0][:], in_=x_rows[0])
         load_scales(0)
         load_words(0)
-        nc.sync.dma_start(out=bias_rows[0:1, 0, :], in_=biases_in[0].unsqueeze(0))
+        nc.sync.dma_start(out=b_embed_sb[:], in_=b_embed.rearrange("(p t) -> p t", t=PACK))
         nc.sync.dma_start(out=pos_sb[:], in_=pos_rows)
         for b in (1, 2):
             nc.sync.dma_start(out=x_sb[b][:], in_=x_rows[b])
@@ -141,7 +146,6 @@ def tile_attention_pa_t_kernel(
 
         x_grouped = {}
         x_mx = {}
-        xe_sb = {}
         xe_grouped = {}
         xe_mx = {}
         qkv_sb = {}
@@ -153,21 +157,28 @@ def tile_attention_pa_t_kernel(
 
         def embed(unit):
             first = PAIR * (unit % 2)
-            xe_pair = work.tile([P, PAIR, WIDTH], BF16, tag="xe_pair")
+            codes, scales = x_mx[unit]
+            grouped = work.tile([P, PAIR, P, PACK], BF16, tag="xe_grouped", align_bytes=64)
             for j in range(PAIR):
-                xe_acc = psum_xe.tile([P, WIDTH], F32, tag="xe_acc")
-                mx_pass(xe_acc, x_mx[unit], j, 0)
+                tokens = slice(j * P, (j + 1) * P)
+                xe_acc = psum_xe.tile([P, PACK, P], F32, tag="xe_acc")
+                for t in range(PACK):
+                    nc.tensor.matmul_mx(
+                        out=xe_acc[:, t, :],
+                        lhsT=we_words[:, t, :].bitcast(FP8X4),
+                        lhsT_scale=we_scales[:, t, :],
+                        rhs=codes[:, tokens].bitcast(FP8X4),
+                        rhs_scale=scales[:, tokens],
+                        start=True,
+                        stop=True,
+                    )
                 nc.vector.tensor_tensor(
-                    out=xe_pair[:, j, :].rearrange("m (u q e) -> m u q e", u=HALVES, e=2),
-                    in0=xe_acc[:].rearrange("m (q u e) -> m u q e", u=HALVES, e=2),
-                    in1=pos_bias[:, first + j, :].rearrange("m (u q e) -> m u q e", u=HALVES, e=2),
+                    out=grouped[:, j, :, :],
+                    in0=xe_acc[:].rearrange("p t m -> p m t"),
+                    in1=pos_bias[:, first + j, :, :],
                     op=ADD,
                 )
-            xe_sb[unit] = xe_pair
-
-        def flip_xe(unit):
-            xe_words = xe_sb[unit][:].bitcast(F32)
-            xe_grouped[unit] = flip(lambda j, u: xe_words[:, j, u * P : (u + 1) * P], "xe")
+            xe_grouped[unit] = grouped
 
         def project(unit, j, o):
             if unit not in qkv_sb:
@@ -201,30 +212,42 @@ def tile_attention_pa_t_kernel(
             nc.tensor.matmul(out=everywhere[:], lhsT=ones[:], rhs=bias_rows[:, w, :], start=True, stop=True)
             return everywhere
 
-        pos_bias = keep.tile([P, TILES, WIDTH], F32)
+        pos_bias = keep.tile([P, TILES, P, PACK], F32)
         bias_sb = keep.tile([P, OUTPUTS, WIDTH], F32)
+        pos_grouped = {}
+
+        def flip_pos(half):
+            pos_words = pos_sb[:].bitcast(F32)
+            first = PAIR * half
+            pos_grouped[half] = flip(lambda j, u: pos_words[:, first + j, u : WIDTH // 2 : HALVES], "pos")
 
         def add_b_embed(i):
             nc.vector.tensor_tensor(
-                out=pos_bias[:, i, :].rearrange("m (u q e) -> m u q e", u=HALVES, e=2),
-                in0=b_embed_everywhere[:].rearrange("m (q u e) -> m u q e", u=HALVES, e=2),
-                in1=pos_sb[:, i, :].rearrange("m (q u e) -> m u q e", u=HALVES, e=2),
+                out=pos_bias[:, i, :, :],
+                in0=pos_grouped[i // PAIR][:, i % PAIR, :, :],
+                in1=b_embed_sb[:].unsqueeze(1).to_broadcast([P, P, PACK]),
                 op=ADD,
             )
 
         flip_x(0)
+        flip_pos(0)
+        nc.vector.tensor_copy(
+            out=we_words[:].bitcast(I32), in_=w_words[:, 0, :].bitcast(I32).rearrange("p (m t) -> p t m", t=PACK)
+        )
+        nc.vector.tensor_copy(
+            out=we_scales[:].rearrange("p t m -> p m t"), in_=w_scales[:, 0, :].rearrange("p (m t) -> p m t", t=PACK)
+        )
         x_mx[0] = quantise(x_grouped[0], "x")
-        b_embed_everywhere = spread(0)
         for i in range(PAIR):
             add_b_embed(i)
 
-        for step in range(-3, UNITS):
-            ahead_x, ahead_embed, ahead_xe = step + 4, step + 3, step + 1
+        for step in range(-2, UNITS):
+            ahead_x, ahead_embed, ahead_xe = step + 3, step + 2, step + 1
             last = step == UNITS - 1
             if ahead_x < UNITS:
                 flip_x(ahead_x)
-            if 0 <= ahead_xe < UNITS:
-                flip_xe(ahead_xe)
+            if ahead_embed == 0:
+                flip_pos(1)
             if 0 <= step:
                 for o in (0, 1, V_OUT):
                     project(step, 0, o)
@@ -242,6 +265,6 @@ def tile_attention_pa_t_kernel(
                 for o in range(OUTPUTS):
                     nc.scalar.copy(out=bias_sb[:, o, :], in_=spread(1 + o)[:])
             if 0 <= step:
-                for o in (V_OUT, 0, 1):
+                for o in (V_OUT, 0, K_OUT):
                     project(step, 1, o)
                 finish(step, 1 if last else 0, PAIR)

@@ -97,18 +97,25 @@ def tile_attention_pa_t_kernel(
             x_batch = keep.tile([P, TILES, WIDTH], BF16, name="x_batch%d" % b)
             x_sb.append(x_batch)
 
-        nc.sync.dma_start(out=x_sb[0][:], in_=x_rows[0])
+        def load_x(b, lo, hi):
+            nc.sync.dma_start(out=x_sb[b][:, lo:hi, :], in_=x_rows[b][:, lo:hi, :])
+
+        def load_pos(lo, hi):
+            nc.sync.dma_start(out=pos_sb[:, lo:hi, :], in_=pos_rows[:, lo:hi, :])
+
+        load_x(0, 0, PAIR)
+        load_pos(0, PAIR)
         load_scales(0)
         load_words(0)
-        nc.sync.dma_start(out=b_embed_sb[:], in_=b_embed.rearrange("(p t) -> p t", t=PACK))
-        nc.sync.dma_start(out=pos_sb[:], in_=pos_rows)
-        for b in (1, 2):
-            nc.sync.dma_start(out=x_sb[b][:], in_=x_rows[b])
+        load_x(0, PAIR, TILES)
+        load_pos(PAIR, TILES)
+        load_x(1, 0, TILES)
         for w in range(1, WEIGHTS):
             load_scales(w)
             load_words(w)
-        for b in range(3, BATCHES):
-            nc.sync.dma_start(out=x_sb[b][:], in_=x_rows[b])
+        for b in range(2, BATCHES):
+            load_x(b, 0, TILES)
+        nc.gpsimd.dma_start(out=b_embed_sb[:], in_=b_embed.rearrange("(p t) -> p t", t=PACK))
         for w in range(1, WEIGHTS):
             nc.gpsimd.dma_start(out=bias_rows[0:1, w, :], in_=biases_in[w].unsqueeze(0))
 
@@ -229,42 +236,49 @@ def tile_attention_pa_t_kernel(
                 op=ADD,
             )
 
-        flip_x(0)
-        flip_pos(0)
-        nc.vector.tensor_copy(
-            out=we_words[:].bitcast(I32), in_=w_words[:, 0, :].bitcast(I32).rearrange("p (m t) -> p t m", t=PACK)
-        )
-        nc.vector.tensor_copy(
-            out=we_scales[:].rearrange("p t m -> p m t"), in_=w_scales[:, 0, :].rearrange("p (m t) -> p m t", t=PACK)
-        )
-        x_mx[0] = quantise(x_grouped[0], "x")
-        for i in range(PAIR):
-            add_b_embed(i)
-
-        for step in range(-2, UNITS):
+        for step in range(-3, UNITS):
             ahead_x, ahead_embed, ahead_xe = step + 3, step + 2, step + 1
             last = step == UNITS - 1
+            if step < 0:
+                if 0 <= ahead_xe:
+                    xe_mx[ahead_xe] = quantise(xe_grouped[ahead_xe], "xe")
+                if ahead_embed == 1:
+                    for i in range(PAIR, TILES):
+                        add_b_embed(i)
+                if 0 <= ahead_embed:
+                    embed(ahead_embed)
+                flip_x(ahead_x)
+                if ahead_x < TILES // PAIR:
+                    flip_pos(ahead_x)
+                if ahead_x == 0:
+                    nc.vector.tensor_copy(
+                        out=we_words[:].bitcast(I32),
+                        in_=w_words[:, 0, :].bitcast(I32).rearrange("p (m t) -> p t m", t=PACK),
+                    )
+                    nc.vector.tensor_copy(
+                        out=we_scales[:].rearrange("p t m -> p m t"),
+                        in_=w_scales[:, 0, :].rearrange("p (m t) -> p m t", t=PACK),
+                    )
+                x_mx[ahead_x] = quantise(x_grouped[ahead_x], "x")
+                if ahead_x == 0:
+                    for i in range(PAIR):
+                        add_b_embed(i)
+                if step == -1:
+                    for o in range(OUTPUTS):
+                        nc.scalar.copy(out=bias_sb[:, o, :], in_=spread(1 + o)[:])
+                continue
             if ahead_x < UNITS:
                 flip_x(ahead_x)
-            if ahead_embed == 0:
-                flip_pos(1)
-            if 0 <= step:
-                for o in (0, 1, V_OUT):
-                    project(step, 0, o)
+            for o in (0, 1, V_OUT):
+                project(step, 0, o)
             if last:
                 finish(step, 0, 1)
             if ahead_x < UNITS:
                 x_mx[ahead_x] = quantise(x_grouped[ahead_x], "x")
-            if 0 <= ahead_xe < UNITS:
+            if ahead_xe < UNITS:
                 xe_mx[ahead_xe] = quantise(xe_grouped[ahead_xe], "xe")
             if ahead_embed < UNITS:
                 embed(ahead_embed)
-            if ahead_embed == 0:
-                for i in range(PAIR, TILES):
-                    add_b_embed(i)
-                for o in range(OUTPUTS):
-                    nc.scalar.copy(out=bias_sb[:, o, :], in_=spread(1 + o)[:])
-            if 0 <= step:
-                for o in (V_OUT, 0, K_OUT):
-                    project(step, 1, o)
-                finish(step, 1 if last else 0, PAIR)
+            for o in (V_OUT, 0, K_OUT):
+                project(step, 1, o)
+            finish(step, 1 if last else 0, PAIR)

@@ -211,8 +211,11 @@ def tile_attention_pa_t_kernel(
                 in1=bias_sb[:, V_OUT, :].unsqueeze(1).to_broadcast([P, hi - lo, WIDTH]),
                 op=ADD,
             )
-            for rows, dest in zip(out_rows, qkv_sb[unit]):
-                nc.sync.dma_start(out=rows[unit // 2][:, first + lo : first + hi, :], in_=dest[:, tiles, :])
+            nc.sync.dma_start(out=out_rows[V_OUT][unit // 2][:, first + lo : first + hi, :], in_=v_sb[:, tiles, :])
+
+        def store_tile(unit, j, o):
+            i = PAIR * (unit % 2) + j
+            nc.sync.dma_start(out=out_rows[o][unit // 2][:, i, :], in_=qkv_sb[unit][o][:, j, :])
 
         def spread(w):
             everywhere = psum_qkv.tile([P, WIDTH], F32, tag="acc")
@@ -271,6 +274,8 @@ def tile_attention_pa_t_kernel(
                 flip_x(ahead_x)
             for o in (0, 1, V_OUT):
                 project(step, 0, o)
+            store_tile(step, 0, 0)
+            store_tile(step, 0, K_OUT)
             if last:
                 finish(step, 0, 1)
             if ahead_x < UNITS:
@@ -281,4 +286,6 @@ def tile_attention_pa_t_kernel(
                 embed(ahead_embed)
             for o in (V_OUT, 0, K_OUT):
                 project(step, 1, o)
+            store_tile(step, 1, 0)
+            store_tile(step, 1, K_OUT)
             finish(step, 1 if last else 0, PAIR)

@@ -201,17 +201,20 @@ def tile_attention_pa_t_kernel(
             else:
                 nc.vector.tensor_tensor(out=dest[:, j, :], in0=acc[:], in1=bias_sb[:, o, :], op=ADD)
 
-        def finish(unit, lo, hi):
-            tiles = slice(lo, hi)
-            first = PAIR * (unit % 2)
+        def add_bv(unit, lo, hi):
             v_sb = qkv_sb[unit][V_OUT]
             nc.gpsimd.tensor_tensor(
-                out=v_sb[:, tiles, :],
-                in0=v_sb[:, tiles, :],
+                out=v_sb[:, lo:hi, :],
+                in0=v_sb[:, lo:hi, :],
                 in1=bias_sb[:, V_OUT, :].unsqueeze(1).to_broadcast([P, hi - lo, WIDTH]),
                 op=ADD,
             )
-            nc.sync.dma_start(out=out_rows[V_OUT][unit // 2][:, first + lo : first + hi, :], in_=v_sb[:, tiles, :])
+
+        def store_v(unit, lo, hi):
+            first = PAIR * (unit % 2)
+            nc.sync.dma_start(
+                out=out_rows[V_OUT][unit // 2][:, first + lo : first + hi, :], in_=qkv_sb[unit][V_OUT][:, lo:hi, :]
+            )
 
         def store_tile(unit, j, o):
             i = PAIR * (unit % 2) + j
@@ -276,8 +279,11 @@ def tile_attention_pa_t_kernel(
                 project(step, 0, o)
             store_tile(step, 0, 0)
             store_tile(step, 0, K_OUT)
+            if 1 <= step:
+                store_v(step - 1, 0, PAIR)
             if last:
-                finish(step, 0, 1)
+                add_bv(step, 0, 1)
+                store_v(step, 0, 1)
             if ahead_x < UNITS:
                 x_mx[ahead_x] = quantise(x_grouped[ahead_x], "x")
             if ahead_xe < UNITS:
@@ -288,4 +294,6 @@ def tile_attention_pa_t_kernel(
                 project(step, 1, o)
             store_tile(step, 1, 0)
             store_tile(step, 1, K_OUT)
-            finish(step, 1 if last else 0, PAIR)
+            add_bv(step, 1 if last else 0, PAIR)
+            if last:
+                store_v(step, 1, PAIR)

from contextlib import ExitStack

import concourse.mybir as mybir
from concourse.masks import make_identity

F32 = mybir.dt.float32
BF16 = mybir.dt.bfloat16
I32 = mybir.dt.int32
U32 = mybir.dt.uint32
U8 = mybir.dt.uint8
FP8X4 = mybir.dt.float8_e4m3fn_x4
ADD = mybir.AluOpType.add

P = 128
BATCHES = 8
POSITIONS = 512
WIDTH = 512
TILES = POSITIONS // P
PAIR = 2
UNITS = BATCHES * TILES // PAIR
PACK = 4
HALVES = 2
WEIGHTS = 4
OUTPUTS = 3
V_OUT = 2
K_OUT = 1

FLOPS = WEIGHTS * 2 * BATCHES * POSITIONS * WIDTH * WIDTH


def tile_attention_pa_t_kernel(
    tc,
    x,
    pos_embed,
    W_embed_words,
    W_embed_scales,
    b_embed,
    Wq_words,
    Wq_scales,
    bq,
    Wk_words,
    Wk_scales,
    bk,
    Wv_words,
    Wv_scales,
    bv,
    out_0,
    out_1,
    out_2,
):
    nc = tc.nc
    words_in = [W_embed_words, Wq_words, Wk_words, Wv_words]
    scales_in = [W_embed_scales, Wq_scales, Wk_scales, Wv_scales]
    biases_in = [b_embed, bq, bk, bv]
    x_rows = x.rearrange("b (p i) c d -> b p i (c d)", i=TILES)
    pos_rows = pos_embed.rearrange("(p i) e -> p i e", i=TILES)
    out_rows = [o.rearrange("b (p i) h d -> b p i (h d)", i=TILES) for o in (out_0, out_1, out_2)]

    with ExitStack() as stack:
        stack.enter_context(tc.manual_schedule())
        keep = stack.enter_context(tc.tile_pool(name="keep", bufs=1))
        work = stack.enter_context(tc.tile_pool(name="work", bufs=3))
        results = stack.enter_context(tc.tile_pool(name="results", bufs=4))
        psum_t = stack.enter_context(tc.psum_pool(name="psum_t", bufs=2))
        psum_xe = stack.enter_context(tc.psum_pool(name="psum_xe", bufs=2))
        psum_qkv = stack.enter_context(tc.psum_pool(name="psum_qkv", bufs=4))

        w_words = keep.tile([P, WEIGHTS, WIDTH], U32, align_bytes=64)
        w_scales = keep.tile([P, WEIGHTS, WIDTH], U8, align_bytes=64)
        bias_rows = keep.tile([P, WEIGHTS, WIDTH], BF16)
        ones = keep.tile([P, P], BF16)
        ident = keep.tile([P, P], F32)
        pos_sb = keep.tile([P, TILES, WIDTH], BF16)
        b_embed_sb = keep.tile([P, PACK], BF16)
        we_words = keep.tile([P, PACK, P], U32, align_bytes=64)
        we_scales = keep.tile([P, PACK, P], U8, align_bytes=64)
        nc.vector.memset(w_scales[:].bitcast(I32), 0)
        nc.vector.memset(bias_rows[:], 0.0)
        nc.vector.memset(ones[:], 1.0)
        make_identity(nc, ident[:])

        def load_scales(w):
            for quadrant in range(4):
                nc.sync.dma_start(
                    out=w_scales[32 * quadrant : 32 * quadrant + 4, w, :].bitcast(I32),
                    in_=scales_in[w][0, 4 * quadrant : 4 * quadrant + 4, :].bitcast(I32),
                )

        def load_words(w):
            nc.sync.dma_start(
                out=w_words[:, w, :].bitcast(I32),
                in_=words_in[w][0].rearrange("p n t -> p (n t)").bitcast(I32),
            )

        x_sb = []
        for b in range(BATCHES):
            x_batch = keep.tile([P, TILES, WIDTH], BF16, name="x_batch%d" % b)
            x_sb.append(x_batch)

        def load_x(b, lo, hi):
            nc.sync.dma_start(out=x_sb[b][:, lo:hi, :], in_=x_rows[b][:, lo:hi, :])

        def load_pos(lo, hi):
            nc.sync.dma_start(out=pos_sb[:, lo:hi, :], in_=pos_rows[:, lo:hi, :])

        load_x(0, 0, PAIR)
        load_pos(0, PAIR)
        load_scales(0)
        load_words(0)
        load_x(0, PAIR, TILES)
        load_pos(PAIR, TILES)
        load_x(1, 0, TILES)
        for w in range(1, WEIGHTS):
            load_scales(w)
            load_words(w)
        for b in range(2, BATCHES):
            load_x(b, 0, TILES)
        nc.gpsimd.dma_start(out=b_embed_sb[:], in_=b_embed.rearrange("(p t) -> p t", t=PACK))
        for w in range(1, WEIGHTS):
            nc.gpsimd.dma_start(out=bias_rows[0:1, w, :], in_=biases_in[w].unsqueeze(0))

        def flip(token_words, kind):
            flipped = psum_t.tile([P, PAIR, HALVES, P], F32, tag="flipped")
            for j in range(PAIR):
                for u in range(HALVES):
                    nc.tensor.transpose(flipped[:, j, u, :], token_words(j, u), ident[:])
            grouped = work.tile([P, PAIR, P, 2 * HALVES], BF16, tag=kind + "_grouped", align_bytes=64)
            nc.scalar.copy(out=grouped[:].bitcast(F32), in_=flipped[:].rearrange("q j u m -> q j m u"))
            return grouped

        def quantise(grouped, kind):
            codes = work.tile([P, PAIR * P], U32, tag=kind + "_codes", align_bytes=64)
            scales = work.tile([P, PAIR * P], U8, tag=kind + "_scales", align_bytes=64)
            nc.vector.quantize_mx(
                out=codes[:].bitcast(FP8X4),
                scales=scales[:],
                in_=grouped[:].rearrange("q j m t -> q (j m t)"),
            )
            return codes, scales

        def mx_pass(acc, operand, j, w):
            codes, scales = operand
            tokens = slice(j * P, (j + 1) * P)
            nc.tensor.matmul_mx(
                out=acc[:],
                lhsT=codes[:, tokens].bitcast(FP8X4),
                lhsT_scale=scales[:, tokens],
                rhs=w_words[:, w, :].bitcast(FP8X4),
                rhs_scale=w_scales[:, w, :],
                start=True,
                stop=True,
            )

        x_grouped = {}
        x_mx = {}
        xe_grouped = {}
        xe_mx = {}
        qkv_sb = {}

        def flip_x(unit):
            x_words = x_sb[unit // 2][:].bitcast(F32)
            first = PAIR * (unit % 2)
            x_grouped[unit] = flip(lambda j, u: x_words[:, first + j, u : WIDTH // 2 : HALVES], "x")

        def embed(unit):
            first = PAIR * (unit % 2)
            codes, scales = x_mx[unit]
            grouped = work.tile([P, PAIR, P, PACK], BF16, tag="xe_grouped", align_bytes=64)
            for j in range(PAIR):
                tokens = slice(j * P, (j + 1) * P)
                xe_acc = psum_xe.tile([P, PACK, P], F32, tag="xe_acc")
                for t in range(PACK):
                    nc.tensor.matmul_mx(
                        out=xe_acc[:, t, :],
                        lhsT=we_words[:, t, :].bitcast(FP8X4),
                        lhsT_scale=we_scales[:, t, :],
                        rhs=codes[:, tokens].bitcast(FP8X4),
                        rhs_scale=scales[:, tokens],
                        start=True,
                        stop=True,
                    )
                nc.vector.tensor_tensor(
                    out=grouped[:, j, :, :],
                    in0=xe_acc[:].rearrange("p t m -> p m t"),
                    in1=pos_bias[:, first + j, :, :],
                    op=ADD,
                )
            xe_grouped[unit] = grouped

        def project(unit, j, o):
            if unit not in qkv_sb:
                q_sb = results.tile([P, PAIR, WIDTH], F32, tag="q_sb")
                k_sb = results.tile([P, PAIR, WIDTH], F32, tag="k_sb")
                v_sb = results.tile([P, PAIR, WIDTH], F32, tag="v_sb")
                qkv_sb[unit] = (q_sb, k_sb, v_sb)
            dest = qkv_sb[unit][o]
            acc = psum_qkv.tile([P, WIDTH], F32, tag="acc")
            mx_pass(acc, xe_mx[unit], j, 1 + o)
            if o == V_OUT:
                nc.scalar.copy(out=dest[:, j, :], in_=acc[:])
            else:
                nc.vector.tensor_tensor(out=dest[:, j, :], in0=acc[:], in1=bias_sb[:, o, :], op=ADD)

        def add_bv(unit, lo, hi):
            v_sb = qkv_sb[unit][V_OUT]
            nc.gpsimd.tensor_tensor(
                out=v_sb[:, lo:hi, :],
                in0=v_sb[:, lo:hi, :],
                in1=bias_sb[:, V_OUT, :].unsqueeze(1).to_broadcast([P, hi - lo, WIDTH]),
                op=ADD,
            )

        def store_v(unit, lo, hi):
            first = PAIR * (unit % 2)
            nc.sync.dma_start(
                out=out_rows[V_OUT][unit // 2][:, first + lo : first + hi, :], in_=qkv_sb[unit][V_OUT][:, lo:hi, :]
            )

        def store_tile(unit, j, o):
            i = PAIR * (unit % 2) + j
            nc.sync.dma_start(out=out_rows[o][unit // 2][:, i, :], in_=qkv_sb[unit][o][:, j, :])

        def spread(w):
            everywhere = psum_qkv.tile([P, WIDTH], F32, tag="acc")
            nc.tensor.matmul(out=everywhere[:], lhsT=ones[:], rhs=bias_rows[:, w, :], start=True, stop=True)
            return everywhere

        pos_bias = keep.tile([P, TILES, P, PACK], F32)
        bias_sb = keep.tile([P, OUTPUTS, WIDTH], F32)
        pos_grouped = {}

        def flip_pos(half):
            pos_words = pos_sb[:].bitcast(F32)
            first = PAIR * half
            pos_grouped[half] = flip(lambda j, u: pos_words[:, first + j, u : WIDTH // 2 : HALVES], "pos")

        def add_b_embed(i):
            nc.vector.tensor_tensor(
                out=pos_bias[:, i, :, :],
                in0=pos_grouped[i // PAIR][:, i % PAIR, :, :],
                in1=b_embed_sb[:].unsqueeze(1).to_broadcast([P, P, PACK]),
                op=ADD,
            )

        for step in range(-3, UNITS):
            ahead_x, ahead_embed, ahead_xe = step + 3, step + 2, step + 1
            last = step == UNITS - 1
            if step < 0:
                if 0 <= ahead_xe:
                    xe_mx[ahead_xe] = quantise(xe_grouped[ahead_xe], "xe")
                if ahead_embed == 1:
                    for i in range(PAIR, TILES):
                        add_b_embed(i)
                if 0 <= ahead_embed:
                    embed(ahead_embed)
                flip_x(ahead_x)
                if ahead_x < TILES // PAIR:
                    flip_pos(ahead_x)
                if ahead_x == 0:
                    nc.vector.tensor_copy(
                        out=we_words[:].bitcast(I32),
                        in_=w_words[:, 0, :].bitcast(I32).rearrange("p (m t) -> p t m", t=PACK),
                    )
                    nc.vector.tensor_copy(
                        out=we_scales[:].rearrange("p t m -> p m t"),
                        in_=w_scales[:, 0, :].rearrange("p (m t) -> p m t", t=PACK),
                    )
                x_mx[ahead_x] = quantise(x_grouped[ahead_x], "x")
                if ahead_x == 0:
                    for i in range(PAIR):
                        add_b_embed(i)
                if step == -1:
                    for o in range(OUTPUTS):
                        nc.scalar.copy(out=bias_sb[:, o, :], in_=spread(1 + o)[:])
                continue
            if ahead_x < UNITS:
                flip_x(ahead_x)
            for o in (0, 1, V_OUT):
                project(step, 0, o)
            store_tile(step, 0, 0)
            store_tile(step, 0, K_OUT)
            if 1 <= step:
                store_v(step - 1, 0, PAIR)
            if last:
                add_bv(step, 0, 1)
                store_v(step, 0, 1)
            if ahead_x < UNITS:
                x_mx[ahead_x] = quantise(x_grouped[ahead_x], "x")
            if ahead_xe < UNITS:
                xe_mx[ahead_xe] = quantise(xe_grouped[ahead_xe], "xe")
            if ahead_embed < UNITS:
                embed(ahead_embed)
            for o in (V_OUT, 0, K_OUT):
                project(step, 1, o)
            store_tile(step, 1, 0)
            store_tile(step, 1, K_OUT)
            add_bv(step, 1 if last else 0, PAIR)
            if last:
                store_v(step, 1, PAIR)
